import numpy as np
import ml_dtypes


def mxq(x, axis, fmt="e4m3"):
    dtype, down = {"e4m3": (ml_dtypes.float8_e4m3fn, 7), "e5m2": (ml_dtypes.float8_e5m2, 14)}[fmt]
    v = np.moveaxis(np.asarray(x, np.float32).astype(ml_dtypes.bfloat16).astype(np.float64), axis, -1)
    blocks = v.reshape(v.shape[:-1] + (-1, 32))
    amax = np.abs(blocks).max(-1, keepdims=True)
    byte = np.maximum(np.where(amax > 0, np.frexp(amax)[1] - 1 + 127, 0) - down, 1)
    scale = np.exp2(byte - 127.0)
    codes = (blocks / scale).astype(np.float32).astype(dtype).astype(np.float64)
    return np.moveaxis((codes * scale).reshape(v.shape), -1, axis)


WIDE = False


def mx_kscale(k):
    if not WIDE:
        return np.ones(k)
    levels = np.array([10, -10, 5, -5, 0])
    if k % 512:
        return np.exp2(np.random.permutation(np.resize(levels, k // 32))).repeat(32)
    a = np.empty((k // 512, 16))
    for p in range(k // 512):
        a[p, :8] = np.random.permutation(np.resize(levels, 8))
        for g in range(8):
            far = levels[np.abs(levels - a[p, g]) >= 10]
            a[p, g + 8] = far[np.random.randint(len(far))]
    return np.exp2(a.ravel()).repeat(32)


BF16 = ml_dtypes.bfloat16


def bf(x):
    return np.asarray(x, np.float32).astype(BF16)


def f64(x):
    return np.asarray(x).astype(np.float64)


B, C, K, BK, BN = 512, 2048, 2048, 1, 16
KEEP = 0.3


def setup_inputs():
    s = mx_kscale(B)[:, None]
    u = mx_kscale(K)
    x0 = bf(np.random.standard_normal((B, C)))
    weight = np.random.uniform(-1.0, 1.0, (K, C)) * 3.2 / np.sqrt(C)
    blk = (np.random.uniform(0.0, 1.0, (K // BK, C // BN)) < KEEP).astype(np.float64)
    mask = np.repeat(np.repeat(blk, BK, axis=0), BN, axis=1)
    w0 = bf(weight * mask)
    bias = bf(np.random.uniform(-1.0, 1.0, K) * 0.5)
    g = bf(np.random.standard_normal((B, K)) * np.exp2(np.random.randint(-6, 1, (B, 1))) * 4.0 / s * u[None, :])
    z = f64(x0) @ f64(w0).T + f64(bias)
    return {"x": bf(f64(x0) * s), "weight": bf(f64(w0) / u[:, None]), "bias": bias,
            "z": np.asarray(z, np.float32), "grad_out": g}


def reference(x, weight, bias, z, grad_out):
    dz = f64(grad_out) * (f64(z) > 0.0)
    dx = mxq(dz, 1, "e5m2") @ mxq(f64(weight), 0, "e4m3")
    dw = mxq(dz, 0, "e5m2").T @ mxq(f64(x), 0, "e4m3")
    return dx, dw

@@ -1,0 +1,236 @@
+from contextlib import ExitStack
+
+import concourse.mybir as mybir
+from concourse.masks import make_identity
+
+TOK, CIN, FEAT = 512, 2048, 2048
+FLOPS = 2 * 2 * TOK * CIN * FEAT
+BYTES = 2 * TOK * CIN + 2 * FEAT * CIN + 4 * TOK * FEAT + 2 * TOK * FEAT + 4 * TOK * CIN + 4 * FEAT * CIN
+
+F32 = mybir.dt.float32
+BF16 = mybir.dt.bfloat16
+U32 = mybir.dt.uint32
+U8 = mybir.dt.uint8
+E4M3 = mybir.dt.float8_e4m3fn_x4
+E5M2 = mybir.dt.float8_e5m2_x4
+ALU = mybir.AluOpType
+
+P = 128
+PACK = 4
+NW = 512
+PASSES = FEAT // (P * PACK)
+NCH = CIN // NW
+MT = FEAT // P
+
+HEAD_BANKS = 14
+STEP_BANKS = 4
+
+
+def tile_sparselinearrelu_v_kernel(tc, x, weight, bias, z, grad_out, out_0, out_1):
+    nc = tc.nc
+    with ExitStack() as ctx:
+        raw = ctx.enter_context(tc.tile_pool(name="raw", bufs=1))
+        grp = ctx.enter_context(tc.tile_pool(name="grp", bufs=4))
+        keep = ctx.enter_context(tc.tile_pool(name="keep", bufs=1))
+        psum = ctx.enter_context(tc.psum_pool(name="psum", bufs=8))
+        ctx.enter_context(tc.manual_schedule())
+
+        def by4(ap):
+            return ap.rearrange("(p j) c -> p j c", j=PACK)
+
+        def cols(i):
+            return slice(NW * i, NW * (i + 1))
+
+        def blk(i):
+            return slice(P * i, P * (i + 1))
+
+        def codes(name):
+            c = keep.tile([P, NW], U32, name=name + "c", align_bytes=64)
+            s = keep.tile([P, NW], U8, name=name + "s", align_bytes=64)
+            return c, s
+
+        x_q = [codes("x%d" % n) for n in range(NCH)]
+        k_q = [codes("k%d" % c) for c in range(PASSES)]
+        t_q = [codes("t%d" % j) for j in range(PACK)]
+        w_q = [[codes("w%d%d" % (g, n)) for n in range(NCH)] for g in range(PASSES)]
+
+        x_v, z_v, g_v, o0_v = by4(x), by4(z), by4(grad_out), by4(out_0)
+        w_tags = ("w0", "w1", "za", "zb")
+        w_raw = [None] * PASSES
+
+        def load_w(g):
+            w_raw[g] = raw.tile([P, PACK, CIN], BF16, name="wraw%d" % g, tag=w_tags[g])
+            nc.sync.dma_start(out=w_raw[g][:], in_=by4(weight[P * PACK * g : P * PACK * (g + 1), :]))
+
+        def load_z(j):
+            nc.sync.dma_start(out=z_raw[j // 2][:, j % 2, :], in_=z_v[:, j, :])
+
+        def load_g(a):
+            nc.sync.dma_start(out=dz[:, 2 * a : 2 * a + 2, :], in_=g_v[:, 2 * a : 2 * a + 2, :])
+
+        load_w(0)
+        x_raw = raw.tile([P, PACK, CIN], BF16, name="xraw", tag="xt")
+        nc.sync.dma_start(out=x_raw[:], in_=x_v)
+        z_raw = [raw.tile([P, 2, FEAT], F32, name="zraw%d" % a, tag=("za", "zb")[a]) for a in range(2)]
+        dz = raw.tile([P, PACK, FEAT], BF16, name="dz", tag="gt")
+        load_z(0)
+        load_g(0)
+        load_z(1)
+        load_g(1)
+        load_z(2)
+        load_z(3)
+        load_w(1)
+
+        ident = keep.tile([P, P], F32, name="ident")
+        make_identity(nc, ident[:])
+        warm = keep.tile([P, 2], F32, name="warm")
+        nc.gpsimd.memset(warm[:, 0:1], 0.0)
+        nc.scalar.copy(out=warm[:, 1:2], in_=warm[:, 0:1])
+
+        def interleave(copy, src, tag):
+            t = grp.tile([P, NW, PACK], BF16, name="grp_" + tag, tag=tag, align_bytes=64)
+            copy(out=t[:], in_=src.rearrange("p j c -> p c j"))
+            return t
+
+        def quantize(t, q, fmt):
+            nc.vector.quantize_mx(out=q[0][:].bitcast(fmt), scales=q[1][:], in_=t[:].rearrange("p c j -> p (c j)"))
+
+        def group_w(g, n):
+            return interleave(nc.vector.tensor_copy, w_raw[g][:, :, cols(n)], "gv")
+
+        def group_dz(c):
+            return interleave(nc.vector.tensor_copy, dz[:, :, cols(c)], "gv")
+
+        def mask(j):
+            nc.vector.scalar_tensor_tensor(out=dz[:, j, :], in0=z_raw[j // 2][:, j % 2, :], scalar=0.0,
+                                           in1=dz[:, j, :], op0=ALU.is_gt, op1=ALU.mult)
+
+        def turn(j):
+            words = dz[:, j, :].bitcast(F32)
+            t = grp.tile([P, NW, PACK], BF16, name="grp_gs", tag="gs", align_bytes=64)
+            t_words = t[:].rearrange("p c j -> p (c j)").bitcast(F32).rearrange("p (g r u) -> p g r u", g=PASSES, u=2)
+            for a in range(2):
+                bank = psum.tile([P, 2, 2, P], F32, name="turned", tag="acc")
+                for gg in range(2):
+                    for u in range(2):
+                        g = 2 * a + gg
+                        nc.tensor.transpose(bank[:, gg, u, :], words[:, 2 * P * g + u : 2 * P * (g + 1) : 2], ident[:])
+                nc.scalar.copy(out=t_words[:, 2 * a : 2 * a + 2], in_=bank[:].rearrange("p g u r -> p g r u"))
+            return t
+
+        def mx(acc, lq, lcol, rq, start, stop):
+            nc.tensor.matmul_mx(out=acc[:], lhsT=lq[0][:, lcol].bitcast(E5M2), lhsT_scale=lq[1][:, lcol],
+                                rhs=rq[0][:].bitcast(E4M3), rhs_scale=rq[1][:], start=start, stop=stop)
+
+        dw_tags = ("w0", "xt", "st")
+        state = {"dw": 0, "pairs": 0, "dw_pair": None, "dx_pair": None, "late": []}
+
+        def stage(tag):
+            return raw.tile([P, 2, 2 * 1024], F32, name="stage", tag=tag)
+
+        def finish(job):
+            eng, dst, acc, store = job
+            if eng == "v":
+                nc.vector.tensor_copy(out=dst, in_=acc[:])
+            else:
+                nc.scalar.copy(out=dst, in_=acc[:])
+            if store is not None:
+                nc.sync.dma_start(out=store[0], in_=store[1])
+
+        def bank_out(eng, dst, acc, store, now):
+            if eng == "v" and not now:
+                state["late"].append((eng, dst, acc, store))
+            else:
+                finish((eng, dst, acc, store))
+
+        def flush_late():
+            for job in state["late"]:
+                finish(job)
+            state["late"] = []
+
+        def dw_bank(eng, now=False):
+            i = state["dw"]
+            state["dw"] = i + 1
+            m, n = i // NCH, i % NCH
+            if i % (2 * NCH) == 0:
+                state["dw_pair"] = stage(dw_tags[state["pairs"] % len(dw_tags)])
+                state["pairs"] += 1
+            pair = state["dw_pair"]
+            acc = psum.tile([P, NW], F32, name="acc", tag="acc")
+            mx(acc, k_q[m // 4], blk(m % 4), x_q[n], True, True)
+            store = (out_1[P * m : P * (m + 1), :], pair[:, m % 2, :]) if n == NCH - 1 else None
+            bank_out(eng, pair[:, m % 2, cols(n)], acc, store, now)
+
+        def dx_group(eng, j, n, now=False):
+            if n % 2 == 0 and j == 0:
+                state["dx_pair"] = stage(("gt", "w1")[n // 2])
+            view = state["dx_pair"][:].rearrange("p a (b c) -> p (a b) c", b=2)
+            acc = psum.tile([P, NW], F32, name="acc", tag="acc")
+            for g in range(PASSES):
+                mx(acc, t_q[j], blk(g), w_q[g][n], g == 0, g == PASSES - 1)
+            h = n // 2
+            store = (o0_v[:, :, 1024 * h : 1024 * (h + 1)], view) if (n % 2 == 1 and j == PACK - 1) else None
+            bank_out(eng, view[:, j, cols(n % 2)], acc, store, now)
+
+        xg = [interleave(nc.scalar.copy, x_raw[:, :, cols(n)], "gs") for n in range(NCH)]
+        wg = [group_w(0, 0), group_w(0, 1)]
+        quantize(wg[0], w_q[0][0], E4M3)
+        wg.append(group_w(0, 2))
+        quantize(wg[1], w_q[0][1], E4M3)
+        wg.append(group_w(0, 3))
+        quantize(wg[2], w_q[0][2], E4M3)
+        quantize(xg[0], x_q[0], E4M3)
+        quantize(wg[3], w_q[0][3], E4M3)
+        mask(0)
+        tg = [turn(0)]
+        quantize(xg[1], x_q[1], E4M3)
+        mask(1)
+        load_w(2)
+        tg.append(turn(1))
+        quantize(xg[2], x_q[2], E4M3)
+        quantize(xg[3], x_q[3], E4M3)
+        mask(2)
+        tg.append(turn(2))
+        quantize(tg[0], t_q[0], E5M2)
+        mask(3)
+        load_w(3)
+        tg.append(turn(3))
+        quantize(tg[1], t_q[1], E5M2)
+
+        units = [(g, n) for n in range(NCH) for g in range(1, PASSES)]
+        dg = group_dz(0)
+        quantize(tg[2], t_q[2], E5M2)
+        quantize(dg, k_q[0], E5M2)
+        dg = group_dz(1)
+        quantize(tg[3], t_q[3], E5M2)
+        quantize(dg, k_q[1], E5M2)
+        dg = group_dz(2)
+        dg3 = group_dz(3)
+        quantize(dg, k_q[2], E5M2)
+        nxt = group_w(units[0][0], units[0][1])
+        quantize(dg3, k_q[3], E5M2)
+
+        for b in range(HEAD_BANKS):
+            dw_bank("s")
+
+        for s in range(len(units)):
+            g, n = units[s]
+            cur = nxt
+            if s + 1 < len(units):
+                nxt = group_w(units[s + 1][0], units[s + 1][1])
+            flush_late()
+            quantize(cur, w_q[g][n], E4M3)
+            ready = []
+            if s >= 3:
+                ready = ((0, 1), (2,), (3,))[s % 3]
+            for b in range(STEP_BANKS):
+                dw_bank("s")
+                if b % 2 == 1 and b // 2 < len(ready):
+                    j = ready[b // 2]
+                    dx_group("s" if j == 0 else "v", j, s // 3 - 1)
+
+        flush_late()
+        for j in range(PACK):
+            dx_group("sv"[j % 2], j, NCH - 1, True)
+        for i in range(MT * NCH - state["dw"]):
+            dw_bank("sv"[i % 2], True)

@@ -22,8 +22,8 @@ PASSES = FEAT // (P * PACK)
 NCH = CIN // NW
 MT = FEAT // P
 
-HEAD_BANKS = 14
-STEP_BANKS = 4
+HEAD_BANKS = 8
+STEP_BANKS = (4, 2)
 
 
 def tile_sparselinearrelu_v_kernel(tc, x, weight, bias, z, grad_out, out_0, out_1):
@@ -59,7 +59,7 @@ def tile_sparselinearrelu_v_kernel(tc, x, weight, bias, z, grad_out, out_0, out_
         w_raw = [None] * PASSES
 
         def load_w(g):
-            w_raw[g] = raw.tile([P, PACK, CIN], BF16, name="wraw%d" % g, tag=w_tags[g])
+            w_raw[g] = raw.tile([P, PACK, CIN], BF16, name="wraw%d" % g, tag=w_tags[g], align_bytes=64)
             nc.sync.dma_start(out=w_raw[g][:], in_=by4(weight[P * PACK * g : P * PACK * (g + 1), :]))
 
         def load_z(j):
@@ -68,17 +68,17 @@ def tile_sparselinearrelu_v_kernel(tc, x, weight, bias, z, grad_out, out_0, out_
         def load_g(a):
             nc.sync.dma_start(out=dz[:, 2 * a : 2 * a + 2, :], in_=g_v[:, 2 * a : 2 * a + 2, :])
 
-        load_w(0)
-        x_raw = raw.tile([P, PACK, CIN], BF16, name="xraw", tag="xt")
+        x_raw = raw.tile([P, PACK, CIN], BF16, name="xraw", tag="xt", align_bytes=64)
         nc.sync.dma_start(out=x_raw[:], in_=x_v)
-        z_raw = [raw.tile([P, 2, FEAT], F32, name="zraw%d" % a, tag=("za", "zb")[a]) for a in range(2)]
-        dz = raw.tile([P, PACK, FEAT], BF16, name="dz", tag="gt")
+        z_raw = [raw.tile([P, 2, FEAT], F32, name="zraw%d" % a, tag=("za", "zb")[a], align_bytes=64) for a in range(2)]
+        dz = raw.tile([P, PACK, FEAT], BF16, name="dz", tag="gt", align_bytes=64)
         load_z(0)
         load_g(0)
         load_z(1)
         load_g(1)
         load_z(2)
         load_z(3)
+        load_w(0)
         load_w(1)
 
         ident = keep.tile([P, P], F32, name="ident")
@@ -87,19 +87,24 @@ def tile_sparselinearrelu_v_kernel(tc, x, weight, bias, z, grad_out, out_0, out_
         nc.gpsimd.memset(warm[:, 0:1], 0.0)
         nc.scalar.copy(out=warm[:, 1:2], in_=warm[:, 0:1])
 
-        def interleave(copy, src, tag):
-            t = grp.tile([P, NW, PACK], BF16, name="grp_" + tag, tag=tag, align_bytes=64)
-            copy(out=t[:], in_=src.rearrange("p j c -> p c j"))
+        head_grp = raw.tile([P, PACK, NW, PACK], BF16, name="headgrp", tag="sg", align_bytes=64)
+
+        def interleave(copy, src, slot=None):
+            if slot is None:
+                t = grp.tile([P, NW, PACK], BF16, name="grp", tag="gv", align_bytes=64)[:]
+            else:
+                t = head_grp[:, slot]
+            copy(out=t, in_=src.rearrange("p j c -> p c j"))
             return t
 
         def quantize(t, q, fmt):
-            nc.vector.quantize_mx(out=q[0][:].bitcast(fmt), scales=q[1][:], in_=t[:].rearrange("p c j -> p (c j)"))
+            nc.vector.quantize_mx(out=q[0][:].bitcast(fmt), scales=q[1][:], in_=t.rearrange("p c j -> p (c j)"))
 
         def group_w(g, n):
-            return interleave(nc.vector.tensor_copy, w_raw[g][:, :, cols(n)], "gv")
+            return interleave(nc.vector.tensor_copy, w_raw[g][:, :, cols(n)])
 
         def group_dz(c):
-            return interleave(nc.vector.tensor_copy, dz[:, :, cols(c)], "gv")
+            return interleave(nc.vector.tensor_copy, dz[:, :, cols(c)])
 
         def mask(j):
             nc.vector.scalar_tensor_tensor(out=dz[:, j, :], in0=z_raw[j // 2][:, j % 2, :], scalar=0.0,
@@ -107,8 +112,8 @@ def tile_sparselinearrelu_v_kernel(tc, x, weight, bias, z, grad_out, out_0, out_
 
         def turn(j):
             words = dz[:, j, :].bitcast(F32)
-            t = grp.tile([P, NW, PACK], BF16, name="grp_gs", tag="gs", align_bytes=64)
-            t_words = t[:].rearrange("p c j -> p (c j)").bitcast(F32).rearrange("p (g r u) -> p g r u", g=PASSES, u=2)
+            t = head_grp[:, j]
+            t_words = t.rearrange("p c j -> p (c j)").bitcast(F32).rearrange("p (g r u) -> p g r u", g=PASSES, u=2)
             for a in range(2):
                 bank = psum.tile([P, 2, 2, P], F32, name="turned", tag="acc")
                 for gg in range(2):
@@ -122,11 +127,11 @@ def tile_sparselinearrelu_v_kernel(tc, x, weight, bias, z, grad_out, out_0, out_
             nc.tensor.matmul_mx(out=acc[:], lhsT=lq[0][:, lcol].bitcast(E5M2), lhsT_scale=lq[1][:, lcol],
                                 rhs=rq[0][:].bitcast(E4M3), rhs_scale=rq[1][:], start=start, stop=stop)
 
-        dw_tags = ("w0", "xt", "st")
+        dw_tags = ("xt", "st", "su", "sg")
         state = {"dw": 0, "pairs": 0, "dw_pair": None, "dx_pair": None, "late": []}
 
         def stage(tag):
-            return raw.tile([P, 2, 2 * 1024], F32, name="stage", tag=tag)
+            return raw.tile([P, 2, 2 * 1024], F32, name="stage", tag=tag, align_bytes=64)
 
         def finish(job):
             eng, dst, acc, store = job
@@ -163,7 +168,7 @@ def tile_sparselinearrelu_v_kernel(tc, x, weight, bias, z, grad_out, out_0, out_
 
         def dx_group(eng, j, n, now=False):
             if n % 2 == 0 and j == 0:
-                state["dx_pair"] = stage(("gt", "w1")[n // 2])
+                state["dx_pair"] = stage(("gt", "w0")[n // 2])
             view = state["dx_pair"][:].rearrange("p a (b c) -> p (a b) c", b=2)
             acc = psum.tile([P, NW], F32, name="acc", tag="acc")
             for g in range(PASSES):
@@ -172,32 +177,29 @@ def tile_sparselinearrelu_v_kernel(tc, x, weight, bias, z, grad_out, out_0, out_
             store = (o0_v[:, :, 1024 * h : 1024 * (h + 1)], view) if (n % 2 == 1 and j == PACK - 1) else None
             bank_out(eng, view[:, j, cols(n % 2)], acc, store, now)
 
-        xg = [interleave(nc.scalar.copy, x_raw[:, :, cols(n)], "gs") for n in range(NCH)]
-        wg = [group_w(0, 0), group_w(0, 1)]
-        quantize(wg[0], w_q[0][0], E4M3)
-        wg.append(group_w(0, 2))
-        quantize(wg[1], w_q[0][1], E4M3)
-        wg.append(group_w(0, 3))
-        quantize(wg[2], w_q[0][2], E4M3)
+        xg = [None] * NCH
+        xg[0] = interleave(nc.scalar.copy, x_raw[:, :, cols(0)], 0)
+        xg[1] = interleave(nc.scalar.copy, x_raw[:, :, cols(1)], 1)
+        xg[2] = interleave(nc.vector.tensor_copy, x_raw[:, :, cols(2)], 2)
+        xg[3] = interleave(nc.vector.tensor_copy, x_raw[:, :, cols(3)], 3)
+        quantize(xg[2], x_q[2], E4M3)
         quantize(xg[0], x_q[0], E4M3)
-        quantize(wg[3], w_q[0][3], E4M3)
+        quantize(xg[3], x_q[3], E4M3)
         mask(0)
-        tg = [turn(0)]
         quantize(xg[1], x_q[1], E4M3)
+        tg = [turn(0)]
         mask(1)
         load_w(2)
         tg.append(turn(1))
-        quantize(xg[2], x_q[2], E4M3)
-        quantize(xg[3], x_q[3], E4M3)
+        quantize(tg[0], t_q[0], E5M2)
         mask(2)
         tg.append(turn(2))
-        quantize(tg[0], t_q[0], E5M2)
+        quantize(tg[1], t_q[1], E5M2)
         mask(3)
         load_w(3)
         tg.append(turn(3))
-        quantize(tg[1], t_q[1], E5M2)
 
-        units = [(g, n) for n in range(NCH) for g in range(1, PASSES)]
+        units = [(g, n) for g in range(PASSES) for n in (0, 1)] + [(g, n) for n in (2, 3) for g in range(PASSES)]
         dg = group_dz(0)
         quantize(tg[2], t_q[2], E5M2)
         quantize(dg, k_q[0], E5M2)
@@ -213,24 +215,23 @@ def tile_sparselinearrelu_v_kernel(tc, x, weight, bias, z, grad_out, out_0, out_
         for b in range(HEAD_BANKS):
             dw_bank("s")
 
+        groups = [(j, n) for n in range(NCH) for j in range(PACK)]
+        done = 0
         for s in range(len(units)):
             g, n = units[s]
             cur = nxt
             if s + 1 < len(units):
                 nxt = group_w(units[s + 1][0], units[s + 1][1])
-            flush_late()
             quantize(cur, w_q[g][n], E4M3)
-            ready = []
-            if s >= 3:
-                ready = ((0, 1), (2,), (3,))[s % 3]
-            for b in range(STEP_BANKS):
+            for b in range(STEP_BANKS[s // 8]):
                 dw_bank("s")
-                if b % 2 == 1 and b // 2 < len(ready):
-                    j = ready[b // 2]
-                    dx_group("s" if j == 0 else "v", j, s // 3 - 1)
+            if s >= 8:
+                for i in range(1 + (s + 1) % 2):
+                    dx_group("s", groups[done][0], groups[done][1])
+                    done += 1
 
-        flush_late()
+        left = MT * NCH - state["dw"]
         for j in range(PACK):
             dx_group("sv"[j % 2], j, NCH - 1, True)
-        for i in range(MT * NCH - state["dw"]):
-            dw_bank("sv"[i % 2], True)
+            for i in range(left // PACK):
+                dw_bank("vs"[(j + i) % 2], True)

@@ -104,7 +104,12 @@ def tile_sparselinearrelu_v_kernel(tc, x, weight, bias, z, grad_out, out_0, out_
             return interleave(nc.vector.tensor_copy, w_raw[g][:, :, cols(n)])
 
         def group_dz(c):
-            return interleave(nc.vector.tensor_copy, dz[:, :, cols(c)])
+            t = grp.tile([P, NW, PACK], BF16, name="grp", tag="gv", align_bytes=64)[:]
+            for q in range(2):
+                f0 = NW * c + 2 * P * q
+                nc.vector.tensor_copy(out=t[:, 2 * P * q : 2 * P * (q + 1), :].rearrange("p (t i) j -> p t i j", t=2),
+                                      in_=dz[:, :, f0 : f0 + 2 * P].rearrange("p j (i t) -> p t i j", t=2))
+            return t
 
         def mask(j):
             nc.vector.scalar_tensor_tensor(out=dz[:, j, :], in0=z_raw[j // 2][:, j % 2, :], scalar=0.0,
@@ -163,7 +168,9 @@ def tile_sparselinearrelu_v_kernel(tc, x, weight, bias, z, grad_out, out_0, out_
             pair = state["dw_pair"]
             acc = psum.tile([P, NW], F32, name="acc", tag="acc")
             mx(acc, k_q[m // 4], blk(m % 4), x_q[n], True, True)
-            store = (out_1[P * m : P * (m + 1), :], pair[:, m % 2, :]) if n == NCH - 1 else None
+            store = None
+            if i % (2 * NCH) == 2 * NCH - 1:
+                store = (out_1[P * (m - 1) : P * (m + 1), :].rearrange("(i t) c -> i t c", t=2), pair[:])
             bank_out(eng, pair[:, m % 2, cols(n)], acc, store, now)
 
         def dx_group(eng, j, n, now=False):

@@ -60,7 +60,8 @@ def tile_sparselinearrelu_v_kernel(tc, x, weight, bias, z, grad_out, out_0, out_
 
         def load_w(g):
             w_raw[g] = raw.tile([P, PACK, CIN], BF16, name="wraw%d" % g, tag=w_tags[g], align_bytes=64)
-            nc.sync.dma_start(out=w_raw[g][:], in_=by4(weight[P * PACK * g : P * PACK * (g + 1), :]))
+            queue = (nc.sync, nc.scalar)[g % 2]
+            queue.dma_start(out=w_raw[g][:], in_=by4(weight[P * PACK * g : P * PACK * (g + 1), :]))
 
         def load_z(j):
             nc.sync.dma_start(out=z_raw[j // 2][:, j % 2, :], in_=z_v[:, j, :])
@@ -79,7 +80,6 @@ def tile_sparselinearrelu_v_kernel(tc, x, weight, bias, z, grad_out, out_0, out_
         load_z(2)
         load_z(3)
         load_w(0)
-        load_w(1)
 
         ident = keep.tile([P, P], F32, name="ident")
         make_identity(nc, ident[:])
@@ -104,12 +104,7 @@ def tile_sparselinearrelu_v_kernel(tc, x, weight, bias, z, grad_out, out_0, out_
             return interleave(nc.vector.tensor_copy, w_raw[g][:, :, cols(n)])
 
         def group_dz(c):
-            t = grp.tile([P, NW, PACK], BF16, name="grp", tag="gv", align_bytes=64)[:]
-            for q in range(2):
-                f0 = NW * c + 2 * P * q
-                nc.vector.tensor_copy(out=t[:, 2 * P * q : 2 * P * (q + 1), :].rearrange("p (t i) j -> p t i j", t=2),
-                                      in_=dz[:, :, f0 : f0 + 2 * P].rearrange("p j (i t) -> p t i j", t=2))
-            return t
+            return interleave(nc.vector.tensor_copy, dz[:, :, cols(c)])
 
         def mask(j):
             nc.vector.scalar_tensor_tensor(out=dz[:, j, :], in0=z_raw[j // 2][:, j % 2, :], scalar=0.0,
@@ -145,7 +140,7 @@ def tile_sparselinearrelu_v_kernel(tc, x, weight, bias, z, grad_out, out_0, out_
             else:
                 nc.scalar.copy(out=dst, in_=acc[:])
             if store is not None:
-                nc.sync.dma_start(out=store[0], in_=store[1])
+                store[2].dma_start(out=store[0], in_=store[1])
 
         def bank_out(eng, dst, acc, store, now):
             if eng == "v" and not now:
@@ -168,9 +163,7 @@ def tile_sparselinearrelu_v_kernel(tc, x, weight, bias, z, grad_out, out_0, out_
             pair = state["dw_pair"]
             acc = psum.tile([P, NW], F32, name="acc", tag="acc")
             mx(acc, k_q[m // 4], blk(m % 4), x_q[n], True, True)
-            store = None
-            if i % (2 * NCH) == 2 * NCH - 1:
-                store = (out_1[P * (m - 1) : P * (m + 1), :].rearrange("(i t) c -> i t c", t=2), pair[:])
+            store = (out_1[P * m : P * (m + 1), :], pair[:, m % 2, :], (nc.scalar, nc.sync)[m % 2]) if n == NCH - 1 else None
             bank_out(eng, pair[:, m % 2, cols(n)], acc, store, now)
 
         def dx_group(eng, j, n, now=False):
@@ -181,7 +174,7 @@ def tile_sparselinearrelu_v_kernel(tc, x, weight, bias, z, grad_out, out_0, out_
             for g in range(PASSES):
                 mx(acc, t_q[j], blk(g), w_q[g][n], g == 0, g == PASSES - 1)
             h = n // 2
-            store = (o0_v[:, :, 1024 * h : 1024 * (h + 1)], view) if (n % 2 == 1 and j == PACK - 1) else None
+            store = (o0_v[:, :, 1024 * h : 1024 * (h + 1)], view, (nc.scalar, nc.sync)[h]) if (n % 2 == 1 and j == PACK - 1) else None
             bank_out(eng, view[:, j, cols(n % 2)], acc, store, now)
 
         xg = [None] * NCH
@@ -201,10 +194,11 @@ def tile_sparselinearrelu_v_kernel(tc, x, weight, bias, z, grad_out, out_0, out_
         quantize(tg[0], t_q[0], E5M2)
         mask(2)
         tg.append(turn(2))
+        load_w(1)
         quantize(tg[1], t_q[1], E5M2)
         mask(3)
-        load_w(3)
         tg.append(turn(3))
+        load_w(3)
 
         units = [(g, n) for g in range(PASSES) for n in (0, 1)] + [(g, n) for n in (2, 3) for g in range(PASSES)]
         dg = group_dz(0)

from contextlib import ExitStack

import concourse.mybir as mybir
from concourse.masks import make_identity

TOK, CIN, FEAT = 512, 2048, 2048
FLOPS = 2 * 2 * TOK * CIN * FEAT
BYTES = 2 * TOK * CIN + 2 * FEAT * CIN + 4 * TOK * FEAT + 2 * TOK * FEAT + 4 * TOK * CIN + 4 * FEAT * CIN

F32 = mybir.dt.float32
BF16 = mybir.dt.bfloat16
U32 = mybir.dt.uint32
U8 = mybir.dt.uint8
E4M3 = mybir.dt.float8_e4m3fn_x4
E5M2 = mybir.dt.float8_e5m2_x4
ALU = mybir.AluOpType

P = 128
PACK = 4
NW = 512
PASSES = FEAT // (P * PACK)
NCH = CIN // NW
MT = FEAT // P

HEAD_BANKS = 8
STEP_BANKS = (4, 2)


def tile_sparselinearrelu_v_kernel(tc, x, weight, bias, z, grad_out, out_0, out_1):
    nc = tc.nc
    with ExitStack() as ctx:
        raw = ctx.enter_context(tc.tile_pool(name="raw", bufs=1))
        grp = ctx.enter_context(tc.tile_pool(name="grp", bufs=4))
        keep = ctx.enter_context(tc.tile_pool(name="keep", bufs=1))
        psum = ctx.enter_context(tc.psum_pool(name="psum", bufs=8))
        ctx.enter_context(tc.manual_schedule())

        def by4(ap):
            return ap.rearrange("(p j) c -> p j c", j=PACK)

        def cols(i):
            return slice(NW * i, NW * (i + 1))

        def blk(i):
            return slice(P * i, P * (i + 1))

        def codes(name):
            c = keep.tile([P, NW], U32, name=name + "c", align_bytes=64)
            s = keep.tile([P, NW], U8, name=name + "s", align_bytes=64)
            return c, s

        x_q = [codes("x%d" % n) for n in range(NCH)]
        k_q = [codes("k%d" % c) for c in range(PASSES)]
        t_q = [codes("t%d" % j) for j in range(PACK)]
        w_q = [[codes("w%d%d" % (g, n)) for n in range(NCH)] for g in range(PASSES)]

        x_v, z_v, g_v, o0_v = by4(x), by4(z), by4(grad_out), by4(out_0)
        w_tags = ("w0", "w1", "za", "zb")
        w_raw = [None] * PASSES

        def load_w(g):
            w_raw[g] = raw.tile([P, PACK, CIN], BF16, name="wraw%d" % g, tag=w_tags[g], align_bytes=64)
            queue = (nc.sync, nc.scalar)[g % 2]
            queue.dma_start(out=w_raw[g][:], in_=by4(weight[P * PACK * g : P * PACK * (g + 1), :]))

        def load_z(j):
            nc.sync.dma_start(out=z_raw[j // 2][:, j % 2, :], in_=z_v[:, j, :])

        def load_g(a):
            nc.sync.dma_start(out=dz[:, 2 * a : 2 * a + 2, :], in_=g_v[:, 2 * a : 2 * a + 2, :])

        x_raw = raw.tile([P, PACK, CIN], BF16, name="xraw", tag="xt", align_bytes=64)
        nc.sync.dma_start(out=x_raw[:], in_=x_v)
        z_raw = [raw.tile([P, 2, FEAT], F32, name="zraw%d" % a, tag=("za", "zb")[a], align_bytes=64) for a in range(2)]
        dz = raw.tile([P, PACK, FEAT], BF16, name="dz", tag="gt", align_bytes=64)
        load_z(0)
        load_g(0)
        load_z(1)
        load_g(1)
        load_z(2)
        load_z(3)
        load_w(0)

        ident = keep.tile([P, P], F32, name="ident")
        make_identity(nc, ident[:])
        warm = keep.tile([P, 2], F32, name="warm")
        nc.gpsimd.memset(warm[:, 0:1], 0.0)
        nc.scalar.copy(out=warm[:, 1:2], in_=warm[:, 0:1])

        head_grp = raw.tile([P, PACK, NW, PACK], BF16, name="headgrp", tag="sg", align_bytes=64)

        def interleave(copy, src, slot=None):
            if slot is None:
                t = grp.tile([P, NW, PACK], BF16, name="grp", tag="gv", align_bytes=64)[:]
            else:
                t = head_grp[:, slot]
            copy(out=t, in_=src.rearrange("p j c -> p c j"))
            return t

        def quantize(t, q, fmt):
            nc.vector.quantize_mx(out=q[0][:].bitcast(fmt), scales=q[1][:], in_=t.rearrange("p c j -> p (c j)"))

        def group_w(g, n):
            return interleave(nc.vector.tensor_copy, w_raw[g][:, :, cols(n)])

        def group_dz(c):
            return interleave(nc.vector.tensor_copy, dz[:, :, cols(c)])

        def mask(j):
            nc.vector.scalar_tensor_tensor(out=dz[:, j, :], in0=z_raw[j // 2][:, j % 2, :], scalar=0.0,
                                           in1=dz[:, j, :], op0=ALU.is_gt, op1=ALU.mult)

        def turn(j):
            words = dz[:, j, :].bitcast(F32)
            t = head_grp[:, j]
            t_words = t.rearrange("p c j -> p (c j)").bitcast(F32).rearrange("p (g r u) -> p g r u", g=PASSES, u=2)
            for a in range(2):
                bank = psum.tile([P, 2, 2, P], F32, name="turned", tag="acc")
                for gg in range(2):
                    for u in range(2):
                        g = 2 * a + gg
                        nc.tensor.transpose(bank[:, gg, u, :], words[:, 2 * P * g + u : 2 * P * (g + 1) : 2], ident[:])
                nc.scalar.copy(out=t_words[:, 2 * a : 2 * a + 2], in_=bank[:].rearrange("p g u r -> p g r u"))
            return t

        def mx(acc, lq, lcol, rq, start, stop):
            nc.tensor.matmul_mx(out=acc[:], lhsT=lq[0][:, lcol].bitcast(E5M2), lhsT_scale=lq[1][:, lcol],
                                rhs=rq[0][:].bitcast(E4M3), rhs_scale=rq[1][:], start=start, stop=stop)

        dw_tags = ("xt", "st", "su", "sg")
        state = {"dw": 0, "pairs": 0, "dw_pair": None, "dx_pair": None, "late": []}

        def stage(tag):
            return raw.tile([P, 2, 2 * 1024], F32, name="stage", tag=tag, align_bytes=64)

        def finish(job):
            eng, dst, acc, store = job
            if eng == "v":
                nc.vector.tensor_copy(out=dst, in_=acc[:])
            else:
                nc.scalar.copy(out=dst, in_=acc[:])
            if store is not None:
                store[2].dma_start(out=store[0], in_=store[1])

        def bank_out(eng, dst, acc, store, now):
            if eng == "v" and not now:
                state["late"].append((eng, dst, acc, store))
            else:
                finish((eng, dst, acc, store))

        def flush_late():
            for job in state["late"]:
                finish(job)
            state["late"] = []

        def dw_bank(eng, now=False):
            i = state["dw"]
            state["dw"] = i + 1
            m, n = i // NCH, i % NCH
            if i % (2 * NCH) == 0:
                state["dw_pair"] = stage(dw_tags[state["pairs"] % len(dw_tags)])
                state["pairs"] += 1
            pair = state["dw_pair"]
            acc = psum.tile([P, NW], F32, name="acc", tag="acc")
            mx(acc, k_q[m // 4], blk(m % 4), x_q[n], True, True)
            store = (out_1[P * m : P * (m + 1), :], pair[:, m % 2, :], (nc.scalar, nc.sync)[m % 2]) if n == NCH - 1 else None
            bank_out(eng, pair[:, m % 2, cols(n)], acc, store, now)

        def dx_group(eng, j, n, now=False):
            if n % 2 == 0 and j == 0:
                state["dx_pair"] = stage(("gt", "w0")[n // 2])
            view = state["dx_pair"][:].rearrange("p a (b c) -> p (a b) c", b=2)
            acc = psum.tile([P, NW], F32, name="acc", tag="acc")
            for g in range(PASSES):
                mx(acc, t_q[j], blk(g), w_q[g][n], g == 0, g == PASSES - 1)
            h = n // 2
            store = (o0_v[:, :, 1024 * h : 1024 * (h + 1)], view, (nc.scalar, nc.sync)[h]) if (n % 2 == 1 and j == PACK - 1) else None
            bank_out(eng, view[:, j, cols(n % 2)], acc, store, now)

        xg = [None] * NCH
        xg[0] = interleave(nc.scalar.copy, x_raw[:, :, cols(0)], 0)
        xg[1] = interleave(nc.scalar.copy, x_raw[:, :, cols(1)], 1)
        xg[2] = interleave(nc.vector.tensor_copy, x_raw[:, :, cols(2)], 2)
        xg[3] = interleave(nc.vector.tensor_copy, x_raw[:, :, cols(3)], 3)
        quantize(xg[2], x_q[2], E4M3)
        quantize(xg[0], x_q[0], E4M3)
        quantize(xg[3], x_q[3], E4M3)
        mask(0)
        quantize(xg[1], x_q[1], E4M3)
        tg = [turn(0)]
        mask(1)
        load_w(2)
        tg.append(turn(1))
        quantize(tg[0], t_q[0], E5M2)
        mask(2)
        tg.append(turn(2))
        load_w(1)
        quantize(tg[1], t_q[1], E5M2)
        mask(3)
        tg.append(turn(3))
        load_w(3)

        units = [(g, n) for g in range(PASSES) for n in (0, 1)] + [(g, n) for n in (2, 3) for g in range(PASSES)]
        dg = group_dz(0)
        quantize(tg[2], t_q[2], E5M2)
        quantize(dg, k_q[0], E5M2)
        dg = group_dz(1)
        quantize(tg[3], t_q[3], E5M2)
        quantize(dg, k_q[1], E5M2)
        dg = group_dz(2)
        dg3 = group_dz(3)
        quantize(dg, k_q[2], E5M2)
        nxt = group_w(units[0][0], units[0][1])
        quantize(dg3, k_q[3], E5M2)

        for b in range(HEAD_BANKS):
            dw_bank("s")

        groups = [(j, n) for n in range(NCH) for j in range(PACK)]
        done = 0
        for s in range(len(units)):
            g, n = units[s]
            cur = nxt
            if s + 1 < len(units):
                nxt = group_w(units[s + 1][0], units[s + 1][1])
            quantize(cur, w_q[g][n], E4M3)
            for b in range(STEP_BANKS[s // 8]):
                dw_bank("s")
            if s >= 8:
                for i in range(1 + (s + 1) % 2):
                    dx_group("s", groups[done][0], groups[done][1])
                    done += 1

        left = MT * NCH - state["dw"]
        for j in range(PACK):
            dx_group("sv"[j % 2], j, NCH - 1, True)
            for i in range(left // PACK):
                dw_bank("vs"[(j + i) % 2], True)
